import numpy as np
import ml_dtypes


def mxq(x, axis, fmt="e4m3"):
    dtype, down = {"e4m3": (ml_dtypes.float8_e4m3fn, 7), "e5m2": (ml_dtypes.float8_e5m2, 14)}[fmt]
    v = np.moveaxis(np.asarray(x, np.float32).astype(ml_dtypes.bfloat16).astype(np.float64), axis, -1)
    blocks = v.reshape(v.shape[:-1] + (-1, 32))
    amax = np.abs(blocks).max(-1, keepdims=True)
    byte = np.maximum(np.where(amax > 0, np.frexp(amax)[1] - 1 + 127, 0) - down, 1)
    scale = np.exp2(byte - 127.0)
    codes = (blocks / scale).astype(np.float32).astype(dtype).astype(np.float64)
    return np.moveaxis((codes * scale).reshape(v.shape), -1, axis)


WIDE = False


def mx_kscale(k):
    if not WIDE:
        return np.ones(k)
    levels = np.array([10, -10, 5, -5, 0])
    a = np.random.permutation(np.resize(levels, k // 512 * 4)).reshape(k // 512, 4)
    idx = np.arange(k)
    return np.exp2(a[idx // 512, idx % 128 // 32])


BF16 = ml_dtypes.bfloat16


def bf(x):
    return np.asarray(x, np.float32).astype(BF16)


def f64(x):
    return np.asarray(x).astype(np.float64)


E2M1 = np.array([0.0, 0.5, 1.0, 1.5, 2.0, 3.0, 4.0, 6.0, -0.0, -0.5, -1.0, -1.5, -2.0, -3.0, -4.0, -6.0])


def pack_weight(w, fmt):
    k, n = w.shape
    w = f64(bf(w)).reshape(k // 32, 32, n)
    amax = np.abs(w).max(1)
    if fmt == "e4m3":
        byte = np.frexp(amax)[1] - 1 + 127 - 7
    else:
        mant, ex = np.frexp(amax / 6.0)
        byte = np.where(mant > 0.5, ex, ex - 1) + 127
    byte = np.clip(np.where(amax > 0, byte, 1), 1, 254)
    scaled = (w * np.exp2(127.0 - byte)[:, None, :]).reshape(k, n).astype(np.float32)
    by_word = np.ascontiguousarray(scaled.reshape(k // 512, 128, 4, n).transpose(0, 1, 3, 2))
    if fmt == "e4m3":
        words = by_word.astype(ml_dtypes.float8_e4m3fn).view(np.uint8)
    else:
        c = by_word.astype(ml_dtypes.float4_e2m1fn).view(np.uint8) & 0xF
        words = c[..., 0::2] | (c[..., 1::2] << 4)
    return np.ascontiguousarray(words), np.ascontiguousarray(byte.astype(np.uint8).reshape(k // 512, 16, n))


def unpack_weight(words, scales, fmt):
    g, p, n, _ = words.shape
    if fmt == "e4m3":
        vals = np.ascontiguousarray(words).view(ml_dtypes.float8_e4m3fn).astype(np.float64)
    else:
        nib = np.empty((g, p, n, 4), np.uint8)
        nib[..., 0::2] = words & 0xF
        nib[..., 1::2] = words >> 4
        vals = E2M1[nib]
    vals = vals * np.repeat(np.exp2(scales.astype(np.float64) - 127.0), 8, axis=1)[..., None]
    return vals.transpose(0, 1, 3, 2).reshape(g * 512, n)


B, T, N, DH, D = 4, 1024, 16, 32, 512
KC = N * DH


def setup_inputs():
    r = np.random.standard_normal
    s = mx_kscale(D)
    t = mx_kscale(KC).reshape(N, DH)
    x = bf(r((B, T, D)) * s)
    wc = r((N, D, DH)) / np.sqrt(D) / s[None, :, None] * t[:, None, :]
    wc_words, wc_scales = pack_weight(wc.reshape(-1, DH), "e4m3")
    b_c = bf(0.1 * r((N, DH)) * t)
    w_k = bf(1.3 / np.sqrt(KC) * r((N, DH, DH, DH)) / t[:, None, None, :])
    return {"normalized_resid_pre": x,
            "W_C_words": wc_words,
            "W_C_scales": wc_scales,
            "b_C": b_c,
            "W_K": w_k}


def reference(normalized_resid_pre, W_C_words, W_C_scales, b_C, W_K):
    x = f64(normalized_resid_pre)
    wc = unpack_weight(W_C_words, W_C_scales, "e4m3").reshape(N, D, DH).transpose(1, 0, 2).reshape(D, KC)
    c = (mxq(x, 2, "e4m3") @ wc) + f64(b_C).reshape(KC)
    wk = f64(W_K).transpose(0, 3, 1, 2).reshape(KC, DH * DH)
    step1 = mxq(c, 2, "e4m3") @ mxq(wk, 0, "e4m3")
    return step1.reshape(B, T, DH, DH)

@@ -1,0 +1,249 @@
+from contextlib import ExitStack
+
+import concourse.mybir as mybir
+from concourse.masks import make_identity
+
+F32 = mybir.dt.float32
+BF16 = mybir.dt.bfloat16
+I32 = mybir.dt.int32
+U32 = mybir.dt.uint32
+U8 = mybir.dt.uint8
+FP8X4 = mybir.dt.float8_e4m3fn_x4
+
+P = 128
+PACK = 4
+TOKENS = 4096
+D_MODEL = 512
+HEADS = 16
+HEAD_DIM = 32
+SUB = HEAD_DIM // PACK
+IJ = HEAD_DIM * HEAD_DIM
+BANK = 512
+HALVES = IJ // BANK
+COLS_PER_ROW = BANK // P
+TILES = 4
+GROUP = TILES * P
+GROUPS = TOKENS // GROUP
+
+FLOPS = 2 * TOKENS * D_MODEL * HEADS * HEAD_DIM + 2 * TOKENS * HEADS * HEAD_DIM * IJ
+
+
+def tile_trittentioncube_pb_t_e_kernel(tc, normalized_resid_pre, W_C_words, W_C_scales, b_C, W_K, out):
+    nc = tc.nc
+
+    x_rows = normalized_resid_pre.rearrange("b t d -> (b t) d").rearrange("(g p r) d -> g p (r d)", p=P, r=TILES)
+    out_rows = out.rearrange("b t i j -> (b t) (i j)").rearrange("(g p r) c -> g p r c", p=P, r=TILES)
+    wk_rows = W_K.rearrange("n i j k -> n (i j) k").rearrange("n (h p c) k -> h p n (c k)", h=HALVES, p=P)
+    wc_word_rows = W_C_words.rearrange("n p k t -> n p (k t)").bitcast(I32).rearrange("n p k -> p n k")
+    wc_scale_rows = W_C_scales.bitcast(I32)
+
+    with ExitStack() as ctx:
+        const = ctx.enter_context(tc.tile_pool(name="const", bufs=1))
+        stage = ctx.enter_context(tc.tile_pool(name="stage", bufs=2))
+        store = ctx.enter_context(tc.tile_pool(name="store", bufs=8))
+        psum_x = ctx.enter_context(tc.psum_pool(name="psum_x", bufs=2))
+        psum_c = ctx.enter_context(tc.psum_pool(name="psum_c", bufs=2))
+        psum_o = ctx.enter_context(tc.psum_pool(name="psum_o", bufs=4))
+
+        ident_f32 = const.tile([P, P], F32, name="ident_f32")
+        ident_bf16 = const.tile([P, P], BF16, name="ident_bf16")
+        x_sb = [const.tile([P, TILES * D_MODEL], BF16, name="x_sb%d" % g) for g in range(GROUPS)]
+        wc_raw = const.tile([P, HEADS * HEAD_DIM], I32, name="wc_raw")
+        wc_words = const.tile([P, PACK * P], I32, name="wc_words", align_bytes=64)
+        wc_planes_raw = const.tile([P, HEADS * HEAD_DIM], U8, name="wc_planes_raw")
+        wc_planes = const.tile([P, PACK * P], U8, name="wc_planes", align_bytes=64)
+        bias_rows = const.tile([P, P], BF16, name="bias_rows")
+        bias = const.tile([P, PACK], F32, name="bias")
+        wk_raw = const.tile([P, HALVES * HEADS * COLS_PER_ROW * HEAD_DIM], BF16, name="wk_raw")
+        wk_sorted = const.tile([P, HALVES * HEADS * COLS_PER_ROW * HEAD_DIM], BF16, name="wk_sorted")
+        wk_grouped = const.tile([P, IJ * PACK], BF16, name="wk_grouped", align_bytes=64)
+        wk_words = const.tile([P, IJ], U32, name="wk_words", align_bytes=64)
+        wk_scales = const.tile([P, IJ], U8, name="wk_scales", align_bytes=64)
+
+        nc.vector.memset(wc_planes_raw[:].bitcast(I32), 0)
+        nc.vector.memset(bias_rows[:], 0.0)
+        make_identity(nc, ident_f32[:])
+        make_identity(nc, ident_bf16[:])
+
+        nc.sync.dma_start(out=x_sb[0][:], in_=x_rows[0])
+        nc.sync.dma_start(out=wc_raw[:].rearrange("p (n k) -> p n k", n=HEADS), in_=wc_word_rows)
+        for quadrant in range(4):
+            nc.sync.dma_start(
+                out=wc_planes_raw[32 * quadrant : 32 * quadrant + 4, :].bitcast(I32).rearrange("j (n w) -> j n w", n=HEADS),
+                in_=wc_scale_rows[:, 4 * quadrant : 4 * quadrant + 4, :].rearrange("n j w -> j n w"),
+            )
+        nc.sync.dma_start(
+            out=bias_rows[0:PACK, :].rearrange("t (n r) -> t n r", r=SUB),
+            in_=b_C.rearrange("n (t r) -> t n r", r=SUB),
+        )
+        for h in range(HALVES):
+            nc.sync.dma_start(
+                out=wk_raw[:].rearrange("p (h n m) -> p h n m", h=HALVES, n=HEADS)[:, h],
+                in_=wk_rows[h],
+            )
+        for g in range(1, GROUPS):
+            nc.sync.dma_start(out=x_sb[g][:], in_=x_rows[g])
+
+        nc.vector.tensor_copy(
+            out=wc_words[:].rearrange("p (t n r) -> p t n r", t=PACK, n=HEADS),
+            in_=wc_raw[:].rearrange("p (n t r) -> p t n r", n=HEADS, t=PACK),
+        )
+        nc.vector.tensor_copy(
+            out=wc_planes[:].bitcast(I32).rearrange("p (t n w) -> p t n w", t=PACK, n=HEADS),
+            in_=wc_planes_raw[:].bitcast(I32).rearrange("p (n t w) -> p t n w", n=HEADS, t=PACK),
+        )
+
+        x_quantised = {}
+        c_tiles = {}
+
+        def transpose_x(g):
+            x_words = x_sb[g][:].bitcast(F32)
+            x_grouped = stage.tile([P, GROUP * PACK], BF16, name="x_grouped", align_bytes=64)
+            grouped_words = x_grouped[:].bitcast(F32).rearrange("p (k u) -> p k u", u=2)
+            words_per_row = D_MODEL // 2
+            for pair in range(TILES // 2):
+                xt = psum_x.tile([P, 2, 2 * P], F32, name="xt")
+                for r in (2 * pair, 2 * pair + 1):
+                    for u in range(2):
+                        nc.tensor.transpose(
+                            xt[:, u, (r % 2) * P : (r % 2 + 1) * P],
+                            x_words[:, r * words_per_row + u : (r + 1) * words_per_row : 2],
+                            ident_f32[:],
+                        )
+                nc.scalar.copy(
+                    out=grouped_words[:, 2 * pair * P : 2 * (pair + 1) * P, :],
+                    in_=xt[:].rearrange("p u k -> p k u"),
+                )
+            return x_grouped
+
+        def quantise_x(g, x_grouped):
+            words = stage.tile([P, GROUP], U32, name="x_codes", align_bytes=64)
+            scales = stage.tile([P, GROUP], U8, name="x_scales", align_bytes=64)
+            nc.vector.quantize_mx(out=words[:].bitcast(FP8X4), scales=scales[:], in_=x_grouped[:])
+            x_quantised[g] = (words, scales)
+
+        def sort_wk(h):
+            src = wk_raw[:].rearrange(
+                "p (h n c u e r) -> p h u c n r e", h=HALVES, n=HEADS, c=COLS_PER_ROW, u=2, e=2, r=SUB
+            )
+            dst = wk_sorted[:].rearrange(
+                "p (h u c n r e) -> p h u c n r e", h=HALVES, n=HEADS, c=COLS_PER_ROW, u=2, e=2, r=SUB
+            )
+            for u in range(2):
+                nc.vector.tensor_copy(out=dst[:, h, u], in_=src[:, h, u])
+
+        def transpose_wk(h):
+            sorted_words = wk_sorted[:].bitcast(F32)
+            grouped_words = wk_grouped[:].bitcast(F32).rearrange(
+                "q (h p a c u) -> q h a p c u", h=HALVES, p=P, a=2, c=2, u=2
+            )
+            for a in range(2):
+                wkt = psum_o.tile([P, 2, 2, P], F32, tag="o", name="wkt")
+                for c in range(2):
+                    for u in range(2):
+                        block = (h * 2 + u) * COLS_PER_ROW + 2 * a + c
+                        nc.tensor.transpose(wkt[:, c, u, :], sorted_words[:, block * P : (block + 1) * P], ident_f32[:])
+                nc.scalar.copy(out=grouped_words[:, h, a], in_=wkt[:].rearrange("q c u p -> q p c u"))
+
+        def quantise_wk(h):
+            nc.vector.quantize_mx(
+                out=wk_words[:, h * BANK : (h + 1) * BANK].bitcast(FP8X4),
+                scales=wk_scales[:, h * BANK : (h + 1) * BANK],
+                in_=wk_grouped[:, h * BANK * PACK : (h + 1) * BANK * PACK],
+            )
+
+        def project(g, r):
+            if r == 0:
+                c_tiles[g] = (
+                    stage.tile([P, GROUP * PACK], BF16, name="c_grouped", align_bytes=64),
+                    stage.tile([P, GROUP], U32, name="c_codes", align_bytes=64),
+                    stage.tile([P, GROUP], U8, name="c_scales", align_bytes=64),
+                )
+            c_grouped = c_tiles[g][0]
+            x_codes, x_scales = x_quantised[g]
+            tokens = slice(r * P, (r + 1) * P)
+            c_ps = psum_c.tile([P, PACK, P], F32, tag="c", name="c_ps")
+            for t in range(PACK):
+                nc.tensor.matmul_mx(
+                    out=c_ps[:, t, :],
+                    lhsT=wc_words[:, t * P : (t + 1) * P].bitcast(FP8X4),
+                    lhsT_scale=wc_planes[:, t * P : (t + 1) * P],
+                    rhs=x_codes[:, tokens].bitcast(FP8X4),
+                    rhs_scale=x_scales[:, tokens],
+                    start=True,
+                    stop=True,
+                )
+            nc.vector.tensor_tensor(
+                out=c_grouped[:].rearrange("p (k t) -> p k t", t=PACK)[:, tokens, :],
+                in0=c_ps[:].rearrange("p t k -> p k t"),
+                in1=bias[:].unsqueeze(1).to_broadcast([P, P, PACK]),
+                op=mybir.AluOpType.add,
+            )
+
+        def quantise_c(g, pair):
+            c_grouped, c_codes, c_scales = c_tiles[g]
+            tokens = slice(2 * pair * P, 2 * (pair + 1) * P)
+            nc.vector.quantize_mx(
+                out=c_codes[:, tokens].bitcast(FP8X4),
+                scales=c_scales[:, tokens],
+                in_=c_grouped[:, 2 * pair * P * PACK : 2 * (pair + 1) * P * PACK],
+            )
+
+        out_tiles = {}
+
+        def contract(g, r):
+            c_codes, c_scales = c_tiles[g][1], c_tiles[g][2]
+            tokens = slice(r * P, (r + 1) * P)
+            if r % 2 == 0:
+                out_tiles[g] = store.tile([P, 2, IJ], F32, name="out_sb")
+            out_sb = out_tiles[g]
+            for h in range(HALVES):
+                o_ps = psum_o.tile([P, BANK], F32, tag="o", name="o_ps")
+                nc.tensor.matmul_mx(
+                    out=o_ps[:],
+                    lhsT=c_codes[:, tokens].bitcast(FP8X4),
+                    lhsT_scale=c_scales[:, tokens],
+                    rhs=wk_words[:, h * BANK : (h + 1) * BANK].bitcast(FP8X4),
+                    rhs_scale=wk_scales[:, h * BANK : (h + 1) * BANK],
+                    start=True,
+                    stop=True,
+                )
+                if r % 2 == 1 and h == 1:
+                    nc.vector.tensor_copy(out=out_sb[:, r % 2, h * BANK : (h + 1) * BANK], in_=o_ps[:])
+                else:
+                    nc.scalar.copy(out=out_sb[:, r % 2, h * BANK : (h + 1) * BANK], in_=o_ps[:])
+            if r % 2 == 1:
+                nc.sync.dma_start(out=out_rows[g][:, r - 1 : r + 1, :], in_=out_sb[:])
+
+        x_grouped = transpose_x(0)
+        bias_t = psum_c.tile([P, P], BF16, tag="c", name="bias_t")
+        nc.tensor.transpose(bias_t[:], bias_rows[:], ident_bf16[:])
+        nc.vector.tensor_copy(out=bias[:], in_=bias_t[:, 0:PACK])
+        quantise_x(0, x_grouped)
+        sort_wk(0)
+        sort_wk(1)
+        project(0, 0)
+        project(0, 1)
+        transpose_wk(0)
+        transpose_wk(1)
+        project(0, 2)
+        quantise_c(0, 0)
+        project(0, 3)
+        quantise_wk(0)
+        quantise_wk(1)
+        x_grouped = transpose_x(1)
+        quantise_x(1, x_grouped)
+
+        for g in range(GROUPS):
+            for r in range(TILES):
+                contract(g, r)
+                if g + 1 < GROUPS:
+                    project(g + 1, r)
+                if r == 0:
+                    quantise_c(g, 1)
+                if r == 1 and g + 2 < GROUPS:
+                    x_grouped = transpose_x(g + 2)
+                if r == 2 and g + 1 < GROUPS:
+                    quantise_c(g + 1, 0)
+                if r == 2 and g + 2 < GROUPS:
+                    quantise_x(g + 2, x_grouped)

@@ -44,6 +44,7 @@ def tile_trittentioncube_pb_t_e_kernel(tc, normalized_resid_pre, W_C_words, W_C_
         psum_x = ctx.enter_context(tc.psum_pool(name="psum_x", bufs=2))
         psum_c = ctx.enter_context(tc.psum_pool(name="psum_c", bufs=2))
         psum_o = ctx.enter_context(tc.psum_pool(name="psum_o", bufs=4))
+        ctx.enter_context(tc.manual_schedule())
 
         ident_f32 = const.tile([P, P], F32, name="ident_f32")
         ident_bf16 = const.tile([P, P], BF16, name="ident_bf16")
@@ -231,19 +232,18 @@ def tile_trittentioncube_pb_t_e_kernel(tc, normalized_resid_pre, W_C_words, W_C_
         project(0, 3)
         quantise_wk(0)
         quantise_wk(1)
+        quantise_c(0, 1)
         x_grouped = transpose_x(1)
         quantise_x(1, x_grouped)
 
         for g in range(GROUPS):
+            if g + 2 < GROUPS:
+                x_grouped = transpose_x(g + 2)
             for r in range(TILES):
-                contract(g, r)
                 if g + 1 < GROUPS:
                     project(g + 1, r)
-                if r == 0:
-                    quantise_c(g, 1)
+                contract(g, r)
+                if r % 2 == 1 and g + 1 < GROUPS:
+                    quantise_c(g + 1, r // 2)
                 if r == 1 and g + 2 < GROUPS:
-                    x_grouped = transpose_x(g + 2)
-                if r == 2 and g + 1 < GROUPS:
-                    quantise_c(g + 1, 0)
-                if r == 2 and g + 2 < GROUPS:
                     quantise_x(g + 2, x_grouped)

@@ -40,7 +40,7 @@ def tile_trittentioncube_pb_t_e_kernel(tc, normalized_resid_pre, W_C_words, W_C_
     with ExitStack() as ctx:
         const = ctx.enter_context(tc.tile_pool(name="const", bufs=1))
         stage = ctx.enter_context(tc.tile_pool(name="stage", bufs=2))
-        store = ctx.enter_context(tc.tile_pool(name="store", bufs=8))
+        store = ctx.enter_context(tc.tile_pool(name="store", bufs=16))
         psum_x = ctx.enter_context(tc.psum_pool(name="psum_x", bufs=2))
         psum_c = ctx.enter_context(tc.psum_pool(name="psum_c", bufs=2))
         psum_o = ctx.enter_context(tc.psum_pool(name="psum_o", bufs=4))
@@ -190,14 +190,10 @@ def tile_trittentioncube_pb_t_e_kernel(tc, normalized_resid_pre, W_C_words, W_C_
                 in_=c_grouped[:, 2 * pair * P * PACK : 2 * (pair + 1) * P * PACK],
             )
 
-        out_tiles = {}
-
         def contract(g, r):
             c_codes, c_scales = c_tiles[g][1], c_tiles[g][2]
             tokens = slice(r * P, (r + 1) * P)
-            if r % 2 == 0:
-                out_tiles[g] = store.tile([P, 2, IJ], F32, name="out_sb")
-            out_sb = out_tiles[g]
+            out_sb = store.tile([P, IJ], F32, name="out_sb")
             for h in range(HALVES):
                 o_ps = psum_o.tile([P, BANK], F32, tag="o", name="o_ps")
                 nc.tensor.matmul_mx(
@@ -210,11 +206,10 @@ def tile_trittentioncube_pb_t_e_kernel(tc, normalized_resid_pre, W_C_words, W_C_
                     stop=True,
                 )
                 if r % 2 == 1 and h == 1:
-                    nc.vector.tensor_copy(out=out_sb[:, r % 2, h * BANK : (h + 1) * BANK], in_=o_ps[:])
+                    nc.vector.tensor_copy(out=out_sb[:, h * BANK : (h + 1) * BANK], in_=o_ps[:])
                 else:
-                    nc.scalar.copy(out=out_sb[:, r % 2, h * BANK : (h + 1) * BANK], in_=o_ps[:])
-            if r % 2 == 1:
-                nc.sync.dma_start(out=out_rows[g][:, r - 1 : r + 1, :], in_=out_sb[:])
+                    nc.scalar.copy(out=out_sb[:, h * BANK : (h + 1) * BANK], in_=o_ps[:])
+            nc.sync.dma_start(out=out_rows[g][:, r, :], in_=out_sb[:])
 
         x_grouped = transpose_x(0)
         bias_t = psum_c.tile([P, P], BF16, tag="c", name="bias_t")

@@ -24,6 +24,8 @@ COLS_PER_ROW = BANK // P
 TILES = 4
 GROUP = TILES * P
 GROUPS = TOKENS // GROUP
+N_TILES = TOKENS // P
+LEAD = 4
 
 FLOPS = 2 * TOKENS * D_MODEL * HEADS * HEAD_DIM + 2 * TOKENS * HEADS * HEAD_DIM * IJ
 
@@ -39,7 +41,8 @@ def tile_trittentioncube_pb_t_e_kernel(tc, normalized_resid_pre, W_C_words, W_C_
 
     with ExitStack() as ctx:
         const = ctx.enter_context(tc.tile_pool(name="const", bufs=1))
-        stage = ctx.enter_context(tc.tile_pool(name="stage", bufs=2))
+        x_stage = ctx.enter_context(tc.tile_pool(name="x_stage", bufs=6))
+        c_stage = ctx.enter_context(tc.tile_pool(name="c_stage", bufs=8))
         store = ctx.enter_context(tc.tile_pool(name="store", bufs=16))
         psum_x = ctx.enter_context(tc.psum_pool(name="psum_x", bufs=2))
         psum_c = ctx.enter_context(tc.psum_pool(name="psum_c", bufs=2))
@@ -94,34 +97,36 @@ def tile_trittentioncube_pb_t_e_kernel(tc, normalized_resid_pre, W_C_words, W_C_
             in_=wc_planes_raw[:].bitcast(I32).rearrange("p (n t w) -> p t n w", n=HEADS, t=PACK),
         )
 
+        x_grouped = {}
         x_quantised = {}
-        c_tiles = {}
+        c_grouped = {}
+        c_quantised = {}
 
         def transpose_x(g):
             x_words = x_sb[g][:].bitcast(F32)
-            x_grouped = stage.tile([P, GROUP * PACK], BF16, name="x_grouped", align_bytes=64)
-            grouped_words = x_grouped[:].bitcast(F32).rearrange("p (k u) -> p k u", u=2)
             words_per_row = D_MODEL // 2
-            for pair in range(TILES // 2):
+            for half in range(2):
+                pair = 2 * g + half
                 xt = psum_x.tile([P, 2, 2 * P], F32, name="xt")
-                for r in (2 * pair, 2 * pair + 1):
+                for i in range(2):
+                    r = 2 * half + i
                     for u in range(2):
                         nc.tensor.transpose(
-                            xt[:, u, (r % 2) * P : (r % 2 + 1) * P],
+                            xt[:, u, i * P : (i + 1) * P],
                             x_words[:, r * words_per_row + u : (r + 1) * words_per_row : 2],
                             ident_f32[:],
                         )
+                x_grouped[pair] = x_stage.tile([P, 2 * P * PACK], BF16, name="x_grouped", align_bytes=64)
                 nc.scalar.copy(
-                    out=grouped_words[:, 2 * pair * P : 2 * (pair + 1) * P, :],
+                    out=x_grouped[pair][:].bitcast(F32).rearrange("p (k u) -> p k u", u=2),
                     in_=xt[:].rearrange("p u k -> p k u"),
                 )
-            return x_grouped
 
-        def quantise_x(g, x_grouped):
-            words = stage.tile([P, GROUP], U32, name="x_codes", align_bytes=64)
-            scales = stage.tile([P, GROUP], U8, name="x_scales", align_bytes=64)
-            nc.vector.quantize_mx(out=words[:].bitcast(FP8X4), scales=scales[:], in_=x_grouped[:])
-            x_quantised[g] = (words, scales)
+        def quantise_x(pair):
+            codes = x_stage.tile([P, 2 * P], U32, name="x_codes", align_bytes=64)
+            scales = x_stage.tile([P, 2 * P], U8, name="x_scales", align_bytes=64)
+            nc.vector.quantize_mx(out=codes[:].bitcast(FP8X4), scales=scales[:], in_=x_grouped[pair][:])
+            x_quantised[pair] = (codes, scales)
 
         def sort_wk(h):
             src = wk_raw[:].rearrange(
@@ -130,8 +135,8 @@ def tile_trittentioncube_pb_t_e_kernel(tc, normalized_resid_pre, W_C_words, W_C_
             dst = wk_sorted[:].rearrange(
                 "p (h u c n r e) -> p h u c n r e", h=HALVES, n=HEADS, c=COLS_PER_ROW, u=2, e=2, r=SUB
             )
-            for u in range(2):
-                nc.vector.tensor_copy(out=dst[:, h, u], in_=src[:, h, u])
+            nc.vector.tensor_copy(out=dst[:, h, 0], in_=src[:, h, 0])
+            nc.scalar.copy(out=dst[:, h, 1], in_=src[:, h, 1])
 
         def transpose_wk(h):
             sorted_words = wk_sorted[:].bitcast(F32)
@@ -153,16 +158,9 @@ def tile_trittentioncube_pb_t_e_kernel(tc, normalized_resid_pre, W_C_words, W_C_
                 in_=wk_grouped[:, h * BANK * PACK : (h + 1) * BANK * PACK],
             )
 
-        def project(g, r):
-            if r == 0:
-                c_tiles[g] = (
-                    stage.tile([P, GROUP * PACK], BF16, name="c_grouped", align_bytes=64),
-                    stage.tile([P, GROUP], U32, name="c_codes", align_bytes=64),
-                    stage.tile([P, GROUP], U8, name="c_scales", align_bytes=64),
-                )
-            c_grouped = c_tiles[g][0]
-            x_codes, x_scales = x_quantised[g]
-            tokens = slice(r * P, (r + 1) * P)
+        def project(j):
+            x_codes, x_scales = x_quantised[j // 2]
+            tokens = slice((j % 2) * P, (j % 2 + 1) * P)
             c_ps = psum_c.tile([P, PACK, P], F32, tag="c", name="c_ps")
             for t in range(PACK):
                 nc.tensor.matmul_mx(
@@ -174,71 +172,71 @@ def tile_trittentioncube_pb_t_e_kernel(tc, normalized_resid_pre, W_C_words, W_C_
                     start=True,
                     stop=True,
                 )
+            c_grouped[j] = c_stage.tile([P, P * PACK], BF16, name="c_grouped", align_bytes=64)
             nc.vector.tensor_tensor(
-                out=c_grouped[:].rearrange("p (k t) -> p k t", t=PACK)[:, tokens, :],
+                out=c_grouped[j][:].rearrange("p (k t) -> p k t", t=PACK),
                 in0=c_ps[:].rearrange("p t k -> p k t"),
                 in1=bias[:].unsqueeze(1).to_broadcast([P, P, PACK]),
                 op=mybir.AluOpType.add,
             )
 
-        def quantise_c(g, pair):
-            c_grouped, c_codes, c_scales = c_tiles[g]
-            tokens = slice(2 * pair * P, 2 * (pair + 1) * P)
-            nc.vector.quantize_mx(
-                out=c_codes[:, tokens].bitcast(FP8X4),
-                scales=c_scales[:, tokens],
-                in_=c_grouped[:, 2 * pair * P * PACK : 2 * (pair + 1) * P * PACK],
-            )
+        def quantise_c(j):
+            codes = c_stage.tile([P, P], U32, name="c_codes", align_bytes=64)
+            scales = c_stage.tile([P, P], U8, name="c_scales", align_bytes=64)
+            nc.vector.quantize_mx(out=codes[:].bitcast(FP8X4), scales=scales[:], in_=c_grouped[j][:])
+            c_quantised[j] = (codes, scales)
 
-        def contract(g, r):
-            c_codes, c_scales = c_tiles[g][1], c_tiles[g][2]
-            tokens = slice(r * P, (r + 1) * P)
+        def contract(j):
+            c_codes, c_scales = c_quantised[j]
             out_sb = store.tile([P, IJ], F32, name="out_sb")
             for h in range(HALVES):
                 o_ps = psum_o.tile([P, BANK], F32, tag="o", name="o_ps")
                 nc.tensor.matmul_mx(
                     out=o_ps[:],
-                    lhsT=c_codes[:, tokens].bitcast(FP8X4),
-                    lhsT_scale=c_scales[:, tokens],
+                    lhsT=c_codes[:].bitcast(FP8X4),
+                    lhsT_scale=c_scales[:],
                     rhs=wk_words[:, h * BANK : (h + 1) * BANK].bitcast(FP8X4),
                     rhs_scale=wk_scales[:, h * BANK : (h + 1) * BANK],
                     start=True,
                     stop=True,
                 )
-                if r % 2 == 1 and h == 1:
+                if h == 1 and (j % 2 == 1 or j + LEAD >= N_TILES):
                     nc.vector.tensor_copy(out=out_sb[:, h * BANK : (h + 1) * BANK], in_=o_ps[:])
                 else:
                     nc.scalar.copy(out=out_sb[:, h * BANK : (h + 1) * BANK], in_=o_ps[:])
-            nc.sync.dma_start(out=out_rows[g][:, r, :], in_=out_sb[:])
+            nc.sync.dma_start(out=out_rows[j // TILES][:, j % TILES, :], in_=out_sb[:])
 
-        x_grouped = transpose_x(0)
+        transpose_x(0)
         bias_t = psum_c.tile([P, P], BF16, tag="c", name="bias_t")
         nc.tensor.transpose(bias_t[:], bias_rows[:], ident_bf16[:])
         nc.vector.tensor_copy(out=bias[:], in_=bias_t[:, 0:PACK])
-        quantise_x(0, x_grouped)
+        quantise_x(0)
+        quantise_x(1)
         sort_wk(0)
+        project(0)
         sort_wk(1)
-        project(0, 0)
-        project(0, 1)
+        project(1)
         transpose_wk(0)
+        quantise_c(0)
+        project(2)
         transpose_wk(1)
-        project(0, 2)
-        quantise_c(0, 0)
-        project(0, 3)
+        quantise_c(1)
+        project(3)
+        quantise_c(2)
+        transpose_x(1)
         quantise_wk(0)
         quantise_wk(1)
-        quantise_c(0, 1)
-        x_grouped = transpose_x(1)
-        quantise_x(1, x_grouped)
+        quantise_x(2)
+        quantise_x(3)
 
-        for g in range(GROUPS):
-            if g + 2 < GROUPS:
-                x_grouped = transpose_x(g + 2)
-            for r in range(TILES):
-                if g + 1 < GROUPS:
-                    project(g + 1, r)
-                contract(g, r)
-                if r % 2 == 1 and g + 1 < GROUPS:
-                    quantise_c(g + 1, r // 2)
-                if r == 1 and g + 2 < GROUPS:
-                    quantise_x(g + 2, x_grouped)
+        for j in range(N_TILES):
+            g, r = divmod(j, TILES)
+            if r == 0 and g + 2 < GROUPS:
+                transpose_x(g + 2)
+            if j + LEAD < N_TILES:
+                project(j + LEAD)
+            contract(j)
+            if j + LEAD - 1 < N_TILES:
+                quantise_c(j + LEAD - 1)
+            if r in (1, 2) and g + 2 < GROUPS:
+                quantise_x(2 * (g + 2) + r - 1)

@@ -50,13 +50,12 @@ def tile_trittentioncube_pb_t_e_kernel(tc, normalized_resid_pre, W_C_words, W_C_
         ctx.enter_context(tc.manual_schedule())
 
         ident_f32 = const.tile([P, P], F32, name="ident_f32")
-        ident_bf16 = const.tile([P, P], BF16, name="ident_bf16")
         x_sb = [const.tile([P, TILES * D_MODEL], BF16, name="x_sb%d" % g) for g in range(GROUPS)]
         wc_raw = const.tile([P, HEADS * HEAD_DIM], I32, name="wc_raw")
         wc_words = const.tile([P, PACK * P], I32, name="wc_words", align_bytes=64)
         wc_planes_raw = const.tile([P, HEADS * HEAD_DIM], U8, name="wc_planes_raw")
         wc_planes = const.tile([P, PACK * P], U8, name="wc_planes", align_bytes=64)
-        bias_rows = const.tile([P, P], BF16, name="bias_rows")
+        bias_bf16 = const.tile([P, PACK], BF16, name="bias_bf16")
         bias = const.tile([P, PACK], F32, name="bias")
         wk_raw = const.tile([P, HALVES * HEADS * COLS_PER_ROW * HEAD_DIM], BF16, name="wk_raw")
         wk_sorted = const.tile([P, HALVES * HEADS * COLS_PER_ROW * HEAD_DIM], BF16, name="wk_sorted")
@@ -65,9 +64,7 @@ def tile_trittentioncube_pb_t_e_kernel(tc, normalized_resid_pre, W_C_words, W_C_
         wk_scales = const.tile([P, IJ], U8, name="wk_scales", align_bytes=64)
 
         nc.vector.memset(wc_planes_raw[:].bitcast(I32), 0)
-        nc.vector.memset(bias_rows[:], 0.0)
         make_identity(nc, ident_f32[:])
-        make_identity(nc, ident_bf16[:])
 
         nc.sync.dma_start(out=x_sb[0][:], in_=x_rows[0])
         nc.sync.dma_start(out=wc_raw[:].rearrange("p (n k) -> p n k", n=HEADS), in_=wc_word_rows)
@@ -76,10 +73,7 @@ def tile_trittentioncube_pb_t_e_kernel(tc, normalized_resid_pre, W_C_words, W_C_
                 out=wc_planes_raw[32 * quadrant : 32 * quadrant + 4, :].bitcast(I32).rearrange("j (n w) -> j n w", n=HEADS),
                 in_=wc_scale_rows[:, 4 * quadrant : 4 * quadrant + 4, :].rearrange("n j w -> j n w"),
             )
-        nc.sync.dma_start(
-            out=bias_rows[0:PACK, :].rearrange("t (n r) -> t n r", r=SUB),
-            in_=b_C.rearrange("n (t r) -> t n r", r=SUB),
-        )
+        nc.sync.dma_start(out=bias_bf16[:], in_=b_C.rearrange("n (r t) -> (n r) t", t=PACK))
         for h in range(HALVES):
             nc.sync.dma_start(
                 out=wk_raw[:].rearrange("p (h n m) -> p h n m", h=HALVES, n=HEADS)[:, h],
@@ -89,12 +83,12 @@ def tile_trittentioncube_pb_t_e_kernel(tc, normalized_resid_pre, W_C_words, W_C_
             nc.sync.dma_start(out=x_sb[g][:], in_=x_rows[g])
 
         nc.vector.tensor_copy(
-            out=wc_words[:].rearrange("p (t n r) -> p t n r", t=PACK, n=HEADS),
-            in_=wc_raw[:].rearrange("p (n t r) -> p t n r", n=HEADS, t=PACK),
+            out=wc_words[:].rearrange("p (t m) -> p t m", t=PACK),
+            in_=wc_raw[:].rearrange("p (m t) -> p t m", t=PACK),
         )
         nc.vector.tensor_copy(
-            out=wc_planes[:].bitcast(I32).rearrange("p (t n w) -> p t n w", t=PACK, n=HEADS),
-            in_=wc_planes_raw[:].bitcast(I32).rearrange("p (n t w) -> p t n w", n=HEADS, t=PACK),
+            out=wc_planes[:].rearrange("p (t m) -> p t m", t=PACK),
+            in_=wc_planes_raw[:].rearrange("p (m t) -> p t m", t=PACK),
         )
 
         x_grouped = {}
@@ -129,11 +123,11 @@ def tile_trittentioncube_pb_t_e_kernel(tc, normalized_resid_pre, W_C_words, W_C_
             x_quantised[pair] = (codes, scales)
 
         def sort_wk(h):
-            src = wk_raw[:].rearrange(
-                "p (h n c u e r) -> p h u c n r e", h=HALVES, n=HEADS, c=COLS_PER_ROW, u=2, e=2, r=SUB
+            src = wk_raw[:].bitcast(F32).rearrange(
+                "p (h n c r u) -> p h u c n r", h=HALVES, n=HEADS, c=COLS_PER_ROW, r=SUB, u=2
             )
-            dst = wk_sorted[:].rearrange(
-                "p (h u c n r e) -> p h u c n r e", h=HALVES, n=HEADS, c=COLS_PER_ROW, u=2, e=2, r=SUB
+            dst = wk_sorted[:].bitcast(F32).rearrange(
+                "p (h u c n r) -> p h u c n r", h=HALVES, n=HEADS, c=COLS_PER_ROW, r=SUB, u=2
             )
             nc.vector.tensor_copy(out=dst[:, h, 0], in_=src[:, h, 0])
             nc.scalar.copy(out=dst[:, h, 1], in_=src[:, h, 1])
@@ -207,9 +201,7 @@ def tile_trittentioncube_pb_t_e_kernel(tc, normalized_resid_pre, W_C_words, W_C_
             nc.sync.dma_start(out=out_rows[j // TILES][:, j % TILES, :], in_=out_sb[:])
 
         transpose_x(0)
-        bias_t = psum_c.tile([P, P], BF16, tag="c", name="bias_t")
-        nc.tensor.transpose(bias_t[:], bias_rows[:], ident_bf16[:])
-        nc.vector.tensor_copy(out=bias[:], in_=bias_t[:, 0:PACK])
+        nc.vector.tensor_copy(out=bias[:], in_=bias_bf16[:])
         quantise_x(0)
         quantise_x(1)
         sort_wk(0)

@@ -50,6 +50,7 @@ def tile_trittentioncube_pb_t_e_kernel(tc, normalized_resid_pre, W_C_words, W_C_
         ctx.enter_context(tc.manual_schedule())
 
         ident_f32 = const.tile([P, P], F32, name="ident_f32")
+        zeros = const.tile([P, BANK], BF16, name="zeros")
         x_sb = [const.tile([P, TILES * D_MODEL], BF16, name="x_sb%d" % g) for g in range(GROUPS)]
         wc_raw = const.tile([P, HEADS * HEAD_DIM], I32, name="wc_raw")
         wc_words = const.tile([P, PACK * P], I32, name="wc_words", align_bytes=64)
@@ -63,6 +64,7 @@ def tile_trittentioncube_pb_t_e_kernel(tc, normalized_resid_pre, W_C_words, W_C_
         wk_words = const.tile([P, IJ], U32, name="wk_words", align_bytes=64)
         wk_scales = const.tile([P, IJ], U8, name="wk_scales", align_bytes=64)
 
+        nc.vector.memset(zeros[:], 0.0)
         nc.vector.memset(wc_planes_raw[:].bitcast(I32), 0)
         make_identity(nc, ident_f32[:])
 
@@ -96,12 +98,18 @@ def tile_trittentioncube_pb_t_e_kernel(tc, normalized_resid_pre, W_C_words, W_C_
         c_grouped = {}
         c_quantised = {}
 
-        def transpose_x(g):
+        def keep_busy(bank, passes):
+            for i in range(passes):
+                nc.tensor.matmul(out=bank, lhsT=zeros[:, 0:P], rhs=zeros[:], start=True, stop=True)
+
+        def transpose_x(g, idle_passes=0):
             x_words = x_sb[g][:].bitcast(F32)
             words_per_row = D_MODEL // 2
             for half in range(2):
                 pair = 2 * g + half
                 xt = psum_x.tile([P, 2, 2 * P], F32, name="xt")
+                if half == 0:
+                    keep_busy(xt[:].rearrange("p u k -> p (u k)"), idle_passes)
                 for i in range(2):
                     r = 2 * half + i
                     for u in range(2):
@@ -152,10 +160,11 @@ def tile_trittentioncube_pb_t_e_kernel(tc, normalized_resid_pre, W_C_words, W_C_
                 in_=wk_grouped[:, h * BANK * PACK : (h + 1) * BANK * PACK],
             )
 
-        def project(j):
+        def project(j, idle_passes=0):
             x_codes, x_scales = x_quantised[j // 2]
             tokens = slice((j % 2) * P, (j % 2 + 1) * P)
             c_ps = psum_c.tile([P, PACK, P], F32, tag="c", name="c_ps")
+            keep_busy(c_ps[:].rearrange("p t k -> p (t k)"), idle_passes)
             for t in range(PACK):
                 nc.tensor.matmul_mx(
                     out=c_ps[:, t, :],
@@ -200,12 +209,12 @@ def tile_trittentioncube_pb_t_e_kernel(tc, normalized_resid_pre, W_C_words, W_C_
                     nc.scalar.copy(out=out_sb[:, h * BANK : (h + 1) * BANK], in_=o_ps[:])
             nc.sync.dma_start(out=out_rows[j // TILES][:, j % TILES, :], in_=out_sb[:])
 
-        transpose_x(0)
+        transpose_x(0, idle_passes=5)
         nc.vector.tensor_copy(out=bias[:], in_=bias_bf16[:])
         quantise_x(0)
         quantise_x(1)
         sort_wk(0)
-        project(0)
+        project(0, idle_passes=3)
         sort_wk(1)
         project(1)
         transpose_wk(0)

@@ -203,7 +203,7 @@ def tile_trittentioncube_pb_t_e_kernel(tc, normalized_resid_pre, W_C_words, W_C_
                     start=True,
                     stop=True,
                 )
-                if h == 1 and (j % 2 == 1 or j + LEAD >= N_TILES):
+                if (HALVES * j + h) % 5 == 4 if j + LEAD < N_TILES else h == 1:
                     nc.vector.tensor_copy(out=out_sb[:, h * BANK : (h + 1) * BANK], in_=o_ps[:])
                 else:
                     nc.scalar.copy(out=out_sb[:, h * BANK : (h + 1) * BANK], in_=o_ps[:])

@@ -44,9 +44,8 @@ def tile_trittentioncube_pb_t_e_kernel(tc, normalized_resid_pre, W_C_words, W_C_
         x_stage = ctx.enter_context(tc.tile_pool(name="x_stage", bufs=6))
         c_stage = ctx.enter_context(tc.tile_pool(name="c_stage", bufs=8))
         store = ctx.enter_context(tc.tile_pool(name="store", bufs=16))
-        psum_x = ctx.enter_context(tc.psum_pool(name="psum_x", bufs=2))
         psum_c = ctx.enter_context(tc.psum_pool(name="psum_c", bufs=2))
-        psum_o = ctx.enter_context(tc.psum_pool(name="psum_o", bufs=4))
+        psum_o = ctx.enter_context(tc.psum_pool(name="psum_o", bufs=6))
         ctx.enter_context(tc.manual_schedule())
 
         ident_f32 = const.tile([P, P], F32, name="ident_f32")
@@ -107,7 +106,7 @@ def tile_trittentioncube_pb_t_e_kernel(tc, normalized_resid_pre, W_C_words, W_C_
             words_per_row = D_MODEL // 2
             for half in range(2):
                 pair = 2 * g + half
-                xt = psum_x.tile([P, 2, 2 * P], F32, name="xt")
+                xt = psum_o.tile([P, 2, 2 * P], F32, tag="o", name="xt")
                 if half == 0:
                     keep_busy(xt[:].rearrange("p u k -> p (u k)"), idle_passes)
                 for i in range(2):

@@ -25,7 +25,7 @@ TILES = 4
 GROUP = TILES * P
 GROUPS = TOKENS // GROUP
 N_TILES = TOKENS // P
-LEAD = 4
+LEAD = 3
 
 FLOPS = 2 * TOKENS * D_MODEL * HEADS * HEAD_DIM + 2 * TOKENS * HEADS * HEAD_DIM * IJ
 
@@ -220,11 +220,9 @@ def tile_trittentioncube_pb_t_e_kernel(tc, normalized_resid_pre, W_C_words, W_C_
         quantise_c(0)
         project(2)
         transpose_wk(1)
-        quantise_c(1)
-        project(3)
-        quantise_c(2)
-        transpose_x(1)
         quantise_wk(0)
+        quantise_c(1)
+        transpose_x(1)
         quantise_wk(1)
         quantise_x(2)
         quantise_x(3)

@@ -25,6 +25,8 @@ TILES = 4
 GROUP = TILES * P
 GROUPS = TOKENS // GROUP
 N_TILES = TOKENS // P
+LOAD_TILES = (4, 4, 4, 4, 16)
+PAIRS_FROM = 24
 LEAD = 3
 
 FLOPS = 2 * TOKENS * D_MODEL * HEADS * HEAD_DIM + 2 * TOKENS * HEADS * HEAD_DIM * IJ
@@ -33,8 +35,18 @@ FLOPS = 2 * TOKENS * D_MODEL * HEADS * HEAD_DIM + 2 * TOKENS * HEADS * HEAD_DIM 
 def tile_trittentioncube_pb_t_e_kernel(tc, normalized_resid_pre, W_C_words, W_C_scales, b_C, W_K, out):
     nc = tc.nc
 
-    x_rows = normalized_resid_pre.rearrange("b t d -> (b t) d").rearrange("(g p r) d -> g p (r d)", p=P, r=TILES)
-    out_rows = out.rearrange("b t i j -> (b t) (i j)").rearrange("(g p r) c -> g p r c", p=P, r=TILES)
+    x_2d = normalized_resid_pre.rearrange("b t d -> (b t) d")
+    out_2d = out.rearrange("b t i j -> (b t) (i j)")
+    first_tile = [sum(LOAD_TILES[:b]) for b in range(len(LOAD_TILES))]
+    load_of = [b for b, rows in enumerate(LOAD_TILES) for i in range(rows)]
+    x_rows = [
+        x_2d[P * first : P * (first + rows), :].rearrange("(p r) d -> p (r d)", r=rows)
+        for first, rows in zip(first_tile, LOAD_TILES)
+    ]
+    out_rows = [
+        out_2d[P * first : P * (first + rows), :].rearrange("(p r) c -> p r c", r=rows)
+        for first, rows in zip(first_tile, LOAD_TILES)
+    ]
     wk_rows = W_K.rearrange("n i j k -> n (i j) k").rearrange("n (h p c) k -> h p n (c k)", h=HALVES, p=P)
     wc_word_rows = W_C_words.rearrange("n p k t -> n p (k t)").bitcast(I32).rearrange("n p k -> p n k")
     wc_scale_rows = W_C_scales.bitcast(I32)
@@ -43,14 +55,14 @@ def tile_trittentioncube_pb_t_e_kernel(tc, normalized_resid_pre, W_C_words, W_C_
         const = ctx.enter_context(tc.tile_pool(name="const", bufs=1))
         x_stage = ctx.enter_context(tc.tile_pool(name="x_stage", bufs=6))
         c_stage = ctx.enter_context(tc.tile_pool(name="c_stage", bufs=8))
-        store = ctx.enter_context(tc.tile_pool(name="store", bufs=16))
+        store = ctx.enter_context(tc.tile_pool(name="store", bufs=8))
         psum_c = ctx.enter_context(tc.psum_pool(name="psum_c", bufs=2))
         psum_o = ctx.enter_context(tc.psum_pool(name="psum_o", bufs=6))
         ctx.enter_context(tc.manual_schedule())
 
         ident_f32 = const.tile([P, P], F32, name="ident_f32")
         zeros = const.tile([P, BANK], BF16, name="zeros")
-        x_sb = [const.tile([P, TILES * D_MODEL], BF16, name="x_sb%d" % g) for g in range(GROUPS)]
+        x_sb = [const.tile([P, rows * D_MODEL], BF16, name="x_sb%d" % b) for b, rows in enumerate(LOAD_TILES)]
         wc_raw = const.tile([P, HEADS * HEAD_DIM], I32, name="wc_raw")
         wc_words = const.tile([P, PACK * P], I32, name="wc_words", align_bytes=64)
         wc_planes_raw = const.tile([P, HEADS * HEAD_DIM], U8, name="wc_planes_raw")
@@ -80,8 +92,8 @@ def tile_trittentioncube_pb_t_e_kernel(tc, normalized_resid_pre, W_C_words, W_C_
                 out=wk_raw[:].rearrange("p (h n m) -> p h n m", h=HALVES, n=HEADS)[:, h],
                 in_=wk_rows[h],
             )
-        for g in range(1, GROUPS):
-            nc.sync.dma_start(out=x_sb[g][:], in_=x_rows[g])
+        for b in range(1, len(LOAD_TILES)):
+            nc.sync.dma_start(out=x_sb[b][:], in_=x_rows[b])
 
         nc.vector.tensor_copy(
             out=wc_words[:].rearrange("p (t m) -> p t m", t=PACK),
@@ -96,13 +108,15 @@ def tile_trittentioncube_pb_t_e_kernel(tc, normalized_resid_pre, W_C_words, W_C_
         x_quantised = {}
         c_grouped = {}
         c_quantised = {}
+        out_pairs = {}
 
         def keep_busy(bank, passes):
             for i in range(passes):
                 nc.tensor.matmul(out=bank, lhsT=zeros[:, 0:P], rhs=zeros[:], start=True, stop=True)
 
         def transpose_x(g, idle_passes=0):
-            x_words = x_sb[g][:].bitcast(F32)
+            b = load_of[TILES * g]
+            x_words = x_sb[b][:].bitcast(F32)
             words_per_row = D_MODEL // 2
             for half in range(2):
                 pair = 2 * g + half
@@ -110,7 +124,7 @@ def tile_trittentioncube_pb_t_e_kernel(tc, normalized_resid_pre, W_C_words, W_C_
                 if half == 0:
                     keep_busy(xt[:].rearrange("p u k -> p (u k)"), idle_passes)
                 for i in range(2):
-                    r = 2 * half + i
+                    r = TILES * g - first_tile[b] + 2 * half + i
                     for u in range(2):
                         nc.tensor.transpose(
                             xt[:, u, i * P : (i + 1) * P],
@@ -190,7 +204,9 @@ def tile_trittentioncube_pb_t_e_kernel(tc, normalized_resid_pre, W_C_words, W_C_
 
         def contract(j):
             c_codes, c_scales = c_quantised[j]
-            out_sb = store.tile([P, IJ], F32, name="out_sb")
+            if j % 2 == 0:
+                out_pairs[j // 2] = store.tile([P, 2, IJ], F32, name="out_sb")
+            out_sb = out_pairs[j // 2]
             for h in range(HALVES):
                 o_ps = psum_o.tile([P, BANK], F32, tag="o", name="o_ps")
                 nc.tensor.matmul_mx(
@@ -203,10 +219,15 @@ def tile_trittentioncube_pb_t_e_kernel(tc, normalized_resid_pre, W_C_words, W_C_
                     stop=True,
                 )
                 if (HALVES * j + h) % 5 == 4 if j + LEAD < N_TILES else h == 1:
-                    nc.vector.tensor_copy(out=out_sb[:, h * BANK : (h + 1) * BANK], in_=o_ps[:])
+                    nc.vector.tensor_copy(out=out_sb[:, j % 2, h * BANK : (h + 1) * BANK], in_=o_ps[:])
                 else:
-                    nc.scalar.copy(out=out_sb[:, h * BANK : (h + 1) * BANK], in_=o_ps[:])
-            nc.sync.dma_start(out=out_rows[j // TILES][:, j % TILES, :], in_=out_sb[:])
+                    nc.scalar.copy(out=out_sb[:, j % 2, h * BANK : (h + 1) * BANK], in_=o_ps[:])
+            b = load_of[j]
+            row = j - first_tile[b]
+            if j < PAIRS_FROM:
+                nc.sync.dma_start(out=out_rows[b][:, row, :], in_=out_sb[:, j % 2, :])
+            elif j % 2 == 1:
+                nc.sync.dma_start(out=out_rows[b][:, row - 1 : row + 1, :], in_=out_sb[:])
 
         transpose_x(0, idle_passes=5)
         nc.vector.tensor_copy(out=bias[:], in_=bias_bf16[:])

@@ -26,7 +26,7 @@ GROUP = TILES * P
 GROUPS = TOKENS // GROUP
 N_TILES = TOKENS // P
 LOAD_TILES = (4, 4, 4, 4, 16)
-PAIRS_FROM = 24
+PAIRS_FROM = 8
 LEAD = 3
 
 FLOPS = 2 * TOKENS * D_MODEL * HEADS * HEAD_DIM + 2 * TOKENS * HEADS * HEAD_DIM * IJ

@@ -27,6 +27,7 @@ GROUPS = TOKENS // GROUP
 N_TILES = TOKENS // P
 LOAD_TILES = (4, 4, 4, 4, 16)
 PAIRS_FROM = 8
+RUN = 4
 LEAD = 3
 
 FLOPS = 2 * TOKENS * D_MODEL * HEADS * HEAD_DIM + 2 * TOKENS * HEADS * HEAD_DIM * IJ
@@ -190,9 +191,9 @@ def tile_trittentioncube_pb_t_e_kernel(tc, normalized_resid_pre, W_C_words, W_C_
                 )
             c_grouped[j] = c_stage.tile([P, P * PACK], BF16, name="c_grouped", align_bytes=64)
             nc.vector.tensor_tensor(
-                out=c_grouped[j][:].rearrange("p (k t) -> p k t", t=PACK),
-                in0=c_ps[:].rearrange("p t k -> p k t"),
-                in1=bias[:].unsqueeze(1).to_broadcast([P, P, PACK]),
+                out=c_grouped[j][:].rearrange("p (k i t) -> p k t i", i=RUN, t=PACK),
+                in0=c_ps[:].rearrange("p t (k i) -> p k t i", i=RUN),
+                in1=bias[:].unsqueeze(1).unsqueeze(3).to_broadcast([P, P // RUN, PACK, RUN]),
                 op=mybir.AluOpType.add,
             )
 

from contextlib import ExitStack

import concourse.mybir as mybir
from concourse.masks import make_identity

F32 = mybir.dt.float32
BF16 = mybir.dt.bfloat16
I32 = mybir.dt.int32
U32 = mybir.dt.uint32
U8 = mybir.dt.uint8
FP8X4 = mybir.dt.float8_e4m3fn_x4

P = 128
PACK = 4
TOKENS = 4096
D_MODEL = 512
HEADS = 16
HEAD_DIM = 32
SUB = HEAD_DIM // PACK
IJ = HEAD_DIM * HEAD_DIM
BANK = 512
HALVES = IJ // BANK
COLS_PER_ROW = BANK // P
TILES = 4
GROUP = TILES * P
GROUPS = TOKENS // GROUP
N_TILES = TOKENS // P
LOAD_TILES = (4, 4, 4, 4, 16)
PAIRS_FROM = 8
RUN = 4
LEAD = 3

FLOPS = 2 * TOKENS * D_MODEL * HEADS * HEAD_DIM + 2 * TOKENS * HEADS * HEAD_DIM * IJ


def tile_trittentioncube_pb_t_e_kernel(tc, normalized_resid_pre, W_C_words, W_C_scales, b_C, W_K, out):
    nc = tc.nc

    x_2d = normalized_resid_pre.rearrange("b t d -> (b t) d")
    out_2d = out.rearrange("b t i j -> (b t) (i j)")
    first_tile = [sum(LOAD_TILES[:b]) for b in range(len(LOAD_TILES))]
    load_of = [b for b, rows in enumerate(LOAD_TILES) for i in range(rows)]
    x_rows = [
        x_2d[P * first : P * (first + rows), :].rearrange("(p r) d -> p (r d)", r=rows)
        for first, rows in zip(first_tile, LOAD_TILES)
    ]
    out_rows = [
        out_2d[P * first : P * (first + rows), :].rearrange("(p r) c -> p r c", r=rows)
        for first, rows in zip(first_tile, LOAD_TILES)
    ]
    wk_rows = W_K.rearrange("n i j k -> n (i j) k").rearrange("n (h p c) k -> h p n (c k)", h=HALVES, p=P)
    wc_word_rows = W_C_words.rearrange("n p k t -> n p (k t)").bitcast(I32).rearrange("n p k -> p n k")
    wc_scale_rows = W_C_scales.bitcast(I32)

    with ExitStack() as ctx:
        const = ctx.enter_context(tc.tile_pool(name="const", bufs=1))
        x_stage = ctx.enter_context(tc.tile_pool(name="x_stage", bufs=6))
        c_stage = ctx.enter_context(tc.tile_pool(name="c_stage", bufs=8))
        store = ctx.enter_context(tc.tile_pool(name="store", bufs=8))
        psum_c = ctx.enter_context(tc.psum_pool(name="psum_c", bufs=2))
        psum_o = ctx.enter_context(tc.psum_pool(name="psum_o", bufs=6))
        ctx.enter_context(tc.manual_schedule())

        ident_f32 = const.tile([P, P], F32, name="ident_f32")
        zeros = const.tile([P, BANK], BF16, name="zeros")
        x_sb = [const.tile([P, rows * D_MODEL], BF16, name="x_sb%d" % b) for b, rows in enumerate(LOAD_TILES)]
        wc_raw = const.tile([P, HEADS * HEAD_DIM], I32, name="wc_raw")
        wc_words = const.tile([P, PACK * P], I32, name="wc_words", align_bytes=64)
        wc_planes_raw = const.tile([P, HEADS * HEAD_DIM], U8, name="wc_planes_raw")
        wc_planes = const.tile([P, PACK * P], U8, name="wc_planes", align_bytes=64)
        bias_bf16 = const.tile([P, PACK], BF16, name="bias_bf16")
        bias = const.tile([P, PACK], F32, name="bias")
        wk_raw = const.tile([P, HALVES * HEADS * COLS_PER_ROW * HEAD_DIM], BF16, name="wk_raw")
        wk_sorted = const.tile([P, HALVES * HEADS * COLS_PER_ROW * HEAD_DIM], BF16, name="wk_sorted")
        wk_grouped = const.tile([P, IJ * PACK], BF16, name="wk_grouped", align_bytes=64)
        wk_words = const.tile([P, IJ], U32, name="wk_words", align_bytes=64)
        wk_scales = const.tile([P, IJ], U8, name="wk_scales", align_bytes=64)

        nc.vector.memset(zeros[:], 0.0)
        nc.vector.memset(wc_planes_raw[:].bitcast(I32), 0)
        make_identity(nc, ident_f32[:])

        nc.sync.dma_start(out=x_sb[0][:], in_=x_rows[0])
        nc.sync.dma_start(out=wc_raw[:].rearrange("p (n k) -> p n k", n=HEADS), in_=wc_word_rows)
        for quadrant in range(4):
            nc.sync.dma_start(
                out=wc_planes_raw[32 * quadrant : 32 * quadrant + 4, :].bitcast(I32).rearrange("j (n w) -> j n w", n=HEADS),
                in_=wc_scale_rows[:, 4 * quadrant : 4 * quadrant + 4, :].rearrange("n j w -> j n w"),
            )
        nc.sync.dma_start(out=bias_bf16[:], in_=b_C.rearrange("n (r t) -> (n r) t", t=PACK))
        for h in range(HALVES):
            nc.sync.dma_start(
                out=wk_raw[:].rearrange("p (h n m) -> p h n m", h=HALVES, n=HEADS)[:, h],
                in_=wk_rows[h],
            )
        for b in range(1, len(LOAD_TILES)):
            nc.sync.dma_start(out=x_sb[b][:], in_=x_rows[b])

        nc.vector.tensor_copy(
            out=wc_words[:].rearrange("p (t m) -> p t m", t=PACK),
            in_=wc_raw[:].rearrange("p (m t) -> p t m", t=PACK),
        )
        nc.vector.tensor_copy(
            out=wc_planes[:].rearrange("p (t m) -> p t m", t=PACK),
            in_=wc_planes_raw[:].rearrange("p (m t) -> p t m", t=PACK),
        )

        x_grouped = {}
        x_quantised = {}
        c_grouped = {}
        c_quantised = {}
        out_pairs = {}

        def keep_busy(bank, passes):
            for i in range(passes):
                nc.tensor.matmul(out=bank, lhsT=zeros[:, 0:P], rhs=zeros[:], start=True, stop=True)

        def transpose_x(g, idle_passes=0):
            b = load_of[TILES * g]
            x_words = x_sb[b][:].bitcast(F32)
            words_per_row = D_MODEL // 2
            for half in range(2):
                pair = 2 * g + half
                xt = psum_o.tile([P, 2, 2 * P], F32, tag="o", name="xt")
                if half == 0:
                    keep_busy(xt[:].rearrange("p u k -> p (u k)"), idle_passes)
                for i in range(2):
                    r = TILES * g - first_tile[b] + 2 * half + i
                    for u in range(2):
                        nc.tensor.transpose(
                            xt[:, u, i * P : (i + 1) * P],
                            x_words[:, r * words_per_row + u : (r + 1) * words_per_row : 2],
                            ident_f32[:],
                        )
                x_grouped[pair] = x_stage.tile([P, 2 * P * PACK], BF16, name="x_grouped", align_bytes=64)
                nc.scalar.copy(
                    out=x_grouped[pair][:].bitcast(F32).rearrange("p (k u) -> p k u", u=2),
                    in_=xt[:].rearrange("p u k -> p k u"),
                )

        def quantise_x(pair):
            codes = x_stage.tile([P, 2 * P], U32, name="x_codes", align_bytes=64)
            scales = x_stage.tile([P, 2 * P], U8, name="x_scales", align_bytes=64)
            nc.vector.quantize_mx(out=codes[:].bitcast(FP8X4), scales=scales[:], in_=x_grouped[pair][:])
            x_quantised[pair] = (codes, scales)

        def sort_wk(h):
            src = wk_raw[:].bitcast(F32).rearrange(
                "p (h n c r u) -> p h u c n r", h=HALVES, n=HEADS, c=COLS_PER_ROW, r=SUB, u=2
            )
            dst = wk_sorted[:].bitcast(F32).rearrange(
                "p (h u c n r) -> p h u c n r", h=HALVES, n=HEADS, c=COLS_PER_ROW, r=SUB, u=2
            )
            nc.vector.tensor_copy(out=dst[:, h, 0], in_=src[:, h, 0])
            nc.scalar.copy(out=dst[:, h, 1], in_=src[:, h, 1])

        def transpose_wk(h):
            sorted_words = wk_sorted[:].bitcast(F32)
            grouped_words = wk_grouped[:].bitcast(F32).rearrange(
                "q (h p a c u) -> q h a p c u", h=HALVES, p=P, a=2, c=2, u=2
            )
            for a in range(2):
                wkt = psum_o.tile([P, 2, 2, P], F32, tag="o", name="wkt")
                for c in range(2):
                    for u in range(2):
                        block = (h * 2 + u) * COLS_PER_ROW + 2 * a + c
                        nc.tensor.transpose(wkt[:, c, u, :], sorted_words[:, block * P : (block + 1) * P], ident_f32[:])
                nc.scalar.copy(out=grouped_words[:, h, a], in_=wkt[:].rearrange("q c u p -> q p c u"))

        def quantise_wk(h):
            nc.vector.quantize_mx(
                out=wk_words[:, h * BANK : (h + 1) * BANK].bitcast(FP8X4),
                scales=wk_scales[:, h * BANK : (h + 1) * BANK],
                in_=wk_grouped[:, h * BANK * PACK : (h + 1) * BANK * PACK],
            )

        def project(j, idle_passes=0):
            x_codes, x_scales = x_quantised[j // 2]
            tokens = slice((j % 2) * P, (j % 2 + 1) * P)
            c_ps = psum_c.tile([P, PACK, P], F32, tag="c", name="c_ps")
            keep_busy(c_ps[:].rearrange("p t k -> p (t k)"), idle_passes)
            for t in range(PACK):
                nc.tensor.matmul_mx(
                    out=c_ps[:, t, :],
                    lhsT=wc_words[:, t * P : (t + 1) * P].bitcast(FP8X4),
                    lhsT_scale=wc_planes[:, t * P : (t + 1) * P],
                    rhs=x_codes[:, tokens].bitcast(FP8X4),
                    rhs_scale=x_scales[:, tokens],
                    start=True,
                    stop=True,
                )
            c_grouped[j] = c_stage.tile([P, P * PACK], BF16, name="c_grouped", align_bytes=64)
            nc.vector.tensor_tensor(
                out=c_grouped[j][:].rearrange("p (k i t) -> p k t i", i=RUN, t=PACK),
                in0=c_ps[:].rearrange("p t (k i) -> p k t i", i=RUN),
                in1=bias[:].unsqueeze(1).unsqueeze(3).to_broadcast([P, P // RUN, PACK, RUN]),
                op=mybir.AluOpType.add,
            )

        def quantise_c(j):
            codes = c_stage.tile([P, P], U32, name="c_codes", align_bytes=64)
            scales = c_stage.tile([P, P], U8, name="c_scales", align_bytes=64)
            nc.vector.quantize_mx(out=codes[:].bitcast(FP8X4), scales=scales[:], in_=c_grouped[j][:])
            c_quantised[j] = (codes, scales)

        def contract(j):
            c_codes, c_scales = c_quantised[j]
            if j % 2 == 0:
                out_pairs[j // 2] = store.tile([P, 2, IJ], F32, name="out_sb")
            out_sb = out_pairs[j // 2]
            for h in range(HALVES):
                o_ps = psum_o.tile([P, BANK], F32, tag="o", name="o_ps")
                nc.tensor.matmul_mx(
                    out=o_ps[:],
                    lhsT=c_codes[:].bitcast(FP8X4),
                    lhsT_scale=c_scales[:],
                    rhs=wk_words[:, h * BANK : (h + 1) * BANK].bitcast(FP8X4),
                    rhs_scale=wk_scales[:, h * BANK : (h + 1) * BANK],
                    start=True,
                    stop=True,
                )
                if (HALVES * j + h) % 5 == 4 if j + LEAD < N_TILES else h == 1:
                    nc.vector.tensor_copy(out=out_sb[:, j % 2, h * BANK : (h + 1) * BANK], in_=o_ps[:])
                else:
                    nc.scalar.copy(out=out_sb[:, j % 2, h * BANK : (h + 1) * BANK], in_=o_ps[:])
            b = load_of[j]
            row = j - first_tile[b]
            if j < PAIRS_FROM:
                nc.sync.dma_start(out=out_rows[b][:, row, :], in_=out_sb[:, j % 2, :])
            elif j % 2 == 1:
                nc.sync.dma_start(out=out_rows[b][:, row - 1 : row + 1, :], in_=out_sb[:])

        transpose_x(0, idle_passes=5)
        nc.vector.tensor_copy(out=bias[:], in_=bias_bf16[:])
        quantise_x(0)
        quantise_x(1)
        sort_wk(0)
        project(0, idle_passes=3)
        sort_wk(1)
        project(1)
        transpose_wk(0)
        quantise_c(0)
        project(2)
        transpose_wk(1)
        quantise_wk(0)
        quantise_c(1)
        transpose_x(1)
        quantise_wk(1)
        quantise_x(2)
        quantise_x(3)

        for j in range(N_TILES):
            g, r = divmod(j, TILES)
            if r == 0 and g + 2 < GROUPS:
                transpose_x(g + 2)
            if j + LEAD < N_TILES:
                project(j + LEAD)
            contract(j)
            if j + LEAD - 1 < N_TILES:
                quantise_c(j + LEAD - 1)
            if r in (1, 2) and g + 2 < GROUPS:
                quantise_x(2 * (g + 2) + r - 1)
